import numpy as np
import ml_dtypes


def mxq(x, axis, fmt="e4m3"):
    dtype, down = {"e4m3": (ml_dtypes.float8_e4m3fn, 7), "e5m2": (ml_dtypes.float8_e5m2, 14)}[fmt]
    v = np.moveaxis(np.asarray(x, np.float32).astype(ml_dtypes.bfloat16).astype(np.float64), axis, -1)
    blocks = v.reshape(v.shape[:-1] + (-1, 32))
    amax = np.abs(blocks).max(-1, keepdims=True)
    byte = np.maximum(np.where(amax > 0, np.frexp(amax)[1] - 1 + 127, 0) - down, 1)
    scale = np.exp2(byte - 127.0)
    codes = (blocks / scale).astype(np.float32).astype(dtype).astype(np.float64)
    return np.moveaxis((codes * scale).reshape(v.shape), -1, axis)


WIDE = False


def mx_kscale(k):
    if not WIDE:
        return np.ones(k)
    levels = np.array([10, -10, 5, -5, 0])
    if k % 512:
        return np.exp2(np.random.permutation(np.resize(levels, k // 32))).repeat(32)
    a = np.empty((k // 512, 16))
    for p in range(k // 512):
        a[p, :8] = np.random.permutation(np.resize(levels, 8))
        for g in range(8):
            far = levels[np.abs(levels - a[p, g]) >= 10]
            a[p, g + 8] = far[np.random.randint(len(far))]
    return np.exp2(a.ravel()).repeat(32)


BF16 = ml_dtypes.bfloat16


def bf(x):
    return np.asarray(x, np.float32).astype(BF16)


def f64(x):
    return np.asarray(x).astype(np.float64)


NB, D1, KB, P, Q, LB, S = 4, 256, 8, 512, 512, 8, 512
D2 = KB * P
R = KB * Q // LB
DO = S * LB


def _blockdiag_butterfly_multiply(x, w1, w2):
    B, n = x.shape
    k, q, p = w1.shape
    l, s, r = w2.shape
    x_r = x.reshape(B, k, p).transpose(1, 0, 2)
    out1 = mxq(x_r, 2, "e4m3") @ mxq(w1, 2, "e4m3").transpose(0, 2, 1)
    out1 = out1.transpose(1, 0, 2).reshape(B, r, l).transpose(2, 0, 1)
    out2 = mxq(out1, 2, "e4m3") @ mxq(w2, 2, "e4m3").transpose(0, 2, 1)
    return out2.transpose(1, 2, 0).reshape(B, s * l)


def setup_inputs():
    s = mx_kscale(P)
    t = mx_kscale(R)
    tf = np.repeat(t, LB).reshape(KB, Q)
    return {"x": bf(np.random.standard_normal((NB, D1, D2)) * np.tile(s, KB)),
            "factorL": bf(np.random.standard_normal((KB, Q, P)) / np.sqrt(P) / s * tf[:, :, None]),
            "factorR": bf(np.random.standard_normal((LB, S, R)) / np.sqrt(R) / t),
            "bias": bf(np.random.standard_normal(DO) * 0.5)}


def reference(x, factorL, factorR, bias):
    b, d1, d2 = x.shape
    out = _blockdiag_butterfly_multiply(f64(x).reshape(-1, d2), f64(factorL), f64(factorR))
    out = out.reshape(b, d1, -1)
    return out + f64(bias)

@@ -1,0 +1,256 @@
+from contextlib import ExitStack
+
+import concourse.mybir as mybir
+from concourse.masks import make_identity
+
+F32 = mybir.dt.float32
+BF16 = mybir.dt.bfloat16
+U32 = mybir.dt.uint32
+U8 = mybir.dt.uint8
+FP8X4 = mybir.dt.float8_e4m3fn_x4
+ADD = mybir.AluOpType.add
+
+P = 128
+TILES = 8
+FLOPS = 2 * 2 * 1024 * 8 * 512 * 512
+
+
+def tile_butterflyblocksparselinear_kernel(tc, x, factorL, factorR, bias, out):
+    nc = tc.nc
+    xf = x.flatten_outer_dims()
+    of = out.flatten_outer_dims()
+    with ExitStack() as ctx:
+        ctx.enter_context(tc.manual_schedule())
+        const = ctx.enter_context(tc.tile_pool(name="const", bufs=1))
+        xpool = ctx.enter_context(tc.tile_pool(name="xpool", bufs=4))
+        wpool = ctx.enter_context(tc.tile_pool(name="wpool", bufs=8))
+        gpool = ctx.enter_context(tc.tile_pool(name="gpool", bufs=2))
+        cpool = ctx.enter_context(tc.tile_pool(name="cpool", bufs=2))
+        opool = ctx.enter_context(tc.tile_pool(name="opool", bufs=6))
+        psum = ctx.enter_context(tc.psum_pool(name="psum", bufs=8))
+
+        ident = const.tile([P, P], F32, name="ident")
+        perm = const.tile([P, P], F32, name="perm")
+        bias_bc = const.tile([P, 4096], BF16, name="bias_bc")
+        l_codes = const.tile([P, 8, 512], U32, name="l_codes", align_bytes=64)
+        l_scales = const.tile([P, 8, 512], U8, name="l_scales", align_bytes=64)
+        r_codes = const.tile([P, 8, 512], U32, name="r_codes", align_bytes=64)
+        r_scales = const.tile([P, 8, 512], U8, name="r_scales", align_bytes=64)
+
+        xraw, xg, xc, xs, hx, hg, gc, gs, ob, wraw, wg, yb = {}, {}, {}, {}, {}, {}, {}, {}, {}, {}, {}, {}
+        copy = {"S": nc.scalar.copy, "V": nc.vector.tensor_copy}
+
+        def load_x(t, pieces=1):
+            xraw[t] = xpool.tile([P, 4096], BF16, name="xraw")
+            w = 4096 // pieces
+            for c in range(pieces):
+                nc.sync.dma_start(out=xraw[t][:, c * w : c * w + w], in_=xf[t * P : (t + 1) * P, c * w : c * w + w])
+
+        def load_l(k):
+            wraw["L", k] = wpool.tile([P, 2048], BF16, name="wraw")
+            nc.sync.dma_start(out=wraw["L", k][:], in_=factorL[k].rearrange("(m a) p -> m (a p)", a=4))
+
+        def load_r(l):
+            wraw["R", l] = wpool.tile([P, 2048], BF16, name="wraw")
+            nc.sync.dma_start(
+                out=wraw["R", l][:].rearrange("m (h c) -> m h c", h=2),
+                in_=factorR[l].rearrange("(h m b) r -> m h (b r)", h=2, b=2),
+            )
+
+        def store(t, sg):
+            nc.sync.dma_start(out=of[t * P : (t + 1) * P, 1024 * sg : 1024 * sg + 1024], in_=ob[t, sg][:])
+
+        def x_bank(t, bk, eng):
+            if bk == 0:
+                xg[t] = gpool.tile([P, 4096], BF16, name="xg", align_bytes=64)
+            words = xraw[t][:].bitcast(F32)
+            tp = psum.tile([P, 512], F32, name="xp", tag="ps")
+            for c in range(4):
+                k, u = 2 * bk + c // 2, c % 2
+                nc.tensor.transpose(tp[:, c * P : (c + 1) * P], words[:, 256 * k + u : 256 * k + 256 : 2], ident[:])
+            copy[eng](
+                out=xg[t][:].bitcast(F32)[:, 512 * bk : 512 * bk + 512].rearrange("p (k c u) -> p k c u", k=2, u=2),
+                in_=tp[:].rearrange("p (k u c) -> p k c u", k=2, u=2),
+            )
+
+        def w_bank(kind, j, half, eng):
+            if half == 0:
+                wg[kind, j] = gpool.tile([P, 2048], BF16, name="wg", bufs=3, align_bytes=64)
+            words = wraw[kind, j][:].bitcast(F32)
+            tp = psum.tile([P, 512], F32, name="wp", tag="ps")
+            for c in range(4):
+                a, u = 2 * half + c // 2, c % 2
+                nc.tensor.transpose(
+                    tp[:, c * P : (c + 1) * P],
+                    words[:, 256 * a + u : 256 * a + 256 : 2],
+                    perm[:] if kind == "L" else ident[:],
+                )
+            dst = wg[kind, j][:].bitcast(F32)[:, 512 * half : 512 * half + 512]
+            if kind == "L":
+                copy[eng](
+                    out=dst.rearrange("p (a n u) -> p a n u", a=2, u=2),
+                    in_=tp[:].rearrange("p (a u n) -> p a n u", a=2, u=2),
+                )
+            else:
+                copy[eng](
+                    out=dst.rearrange("p (m b u) -> p m b u", b=2, u=2),
+                    in_=tp[:].rearrange("p (b u m) -> p m b u", b=2, u=2),
+                )
+
+        def g_bank(t, bk, eng):
+            if bk == 0:
+                hg[t] = gpool.tile([P, 4096], BF16, name="hg", align_bytes=64)
+            words = hx[t][:].bitcast(F32)
+            tp = psum.tile([P, 512], F32, name="gp", tag="ps")
+            for c in range(4):
+                n = 4 * bk + c
+                nc.tensor.transpose(tp[:, c * P : (c + 1) * P], words[:, n * P : (n + 1) * P], ident[:])
+            copy[eng](
+                out=hg[t][:].bitcast(F32)[:, 512 * bk : 512 * bk + 512].rearrange("p (l c v) -> p l c v", l=2, v=2),
+                in_=tp[:].rearrange("p (l v c) -> p l c v", l=2, v=2),
+            )
+
+        def quant_x(t, half=None):
+            if half in (None, 0):
+                xc[t] = cpool.tile([P, 1024], U32, name="xc", align_bytes=64)
+                xs[t] = cpool.tile([P, 1024], U8, name="xs", align_bytes=64)
+            a, b = (0, 1024) if half is None else (512 * half, 512 * half + 512)
+            nc.vector.quantize_mx(out=xc[t][:, a:b].bitcast(FP8X4), scales=xs[t][:, a:b], in_=xg[t][:, 4 * a : 4 * b])
+
+        def quant_w(kind, j):
+            codes, scales = (l_codes, l_scales) if kind == "L" else (r_codes, r_scales)
+            nc.vector.quantize_mx(out=codes[:, j, :].bitcast(FP8X4), scales=scales[:, j, :], in_=wg[kind, j][:])
+
+        def quant_g(t):
+            gc[t] = cpool.tile([P, 1024], U32, name="gc", align_bytes=64)
+            gs[t] = cpool.tile([P, 1024], U8, name="gs", align_bytes=64)
+            nc.vector.quantize_mx(out=gc[t][:].bitcast(FP8X4), scales=gs[t][:], in_=hg[t][:])
+
+        def h_bank(t, k, eng):
+            if k == 0:
+                hx[t] = gpool.tile([P, 4096], BF16, name="hx", align_bytes=64)
+            hb = psum.tile([P, 512], F32, name="hb", tag="ps")
+            nc.tensor.matmul_mx(
+                out=hb[:],
+                lhsT=xc[t][:, k * P : (k + 1) * P].bitcast(FP8X4),
+                lhsT_scale=xs[t][:, k * P : (k + 1) * P],
+                rhs=l_codes[:, k, :].bitcast(FP8X4),
+                rhs_scale=l_scales[:, k, :],
+                start=True,
+                stop=True,
+            )
+            copy[eng](
+                out=hx[t][:].rearrange("p (n k i) -> p n k i", k=8, i=32)[:, :, k, :],
+                in_=hb[:].rearrange("p (n i) -> p n i", i=32),
+            )
+
+        def y_mm(t, n):
+            sg, lh = n // 2, n % 2
+            yb[t, n] = psum.tile([P, 512], F32, name="yb", tag="ps")
+            for a in range(4):
+                c = 2 * a + lh
+                nc.tensor.matmul_mx(
+                    out=yb[t, n][:, a * P : (a + 1) * P],
+                    lhsT=gc[t][:, c * P : (c + 1) * P].bitcast(FP8X4),
+                    lhsT_scale=gs[t][:, c * P : (c + 1) * P],
+                    rhs=r_codes[:, 4 * lh + a, sg * P : (sg + 1) * P].bitcast(FP8X4),
+                    rhs_scale=r_scales[:, 4 * lh + a, sg * P : (sg + 1) * P],
+                    start=True,
+                    stop=True,
+                )
+
+        def y_out(t, n):
+            sg, lh = n // 2, n % 2
+            if lh == 0:
+                ob[t, sg] = opool.tile([P, 1024], F32, name="ob")
+            cols = slice(4 * lh, 4 * lh + 4)
+            nc.vector.tensor_tensor(
+                out=ob[t, sg][:].rearrange("p (s l) -> p s l", l=8)[:, :, cols],
+                in0=yb[t, n][:].rearrange("p (l s) -> p s l", l=4),
+                in1=bias_bc[:, 1024 * sg : 1024 * sg + 1024].rearrange("p (s l) -> p s l", l=8)[:, :, cols],
+                op=ADD,
+            )
+            if lh == 1:
+                store(t, sg)
+
+        load_x(0, 4)
+        for k in range(8):
+            load_l(k)
+        load_x(1)
+        make_identity(nc, ident[:])
+        for lh in range(2):
+            nc.vector.tensor_copy(
+                out=perm[:, 64 * lh : 64 * lh + 64].rearrange("p (v i e) -> p v i e", v=2, e=2),
+                in_=ident[:].rearrange("p (i v e b) -> p b v i e", v=2, e=2, b=2)[:, lh],
+            )
+        for bk in range(4):
+            x_bank(0, bk, "SV"[bk % 2])
+            if bk % 2:
+                quant_x(0, bk // 2)
+        for i in range(4):
+            for k in (2 * i, 2 * i + 1):
+                w_bank("L", k, 0, "S")
+                w_bank("L", k, 1, "V")
+                if k:
+                    quant_w("L", k - 1)
+                load_r(k)
+            if i:
+                h_bank(0, 2 * i - 2, "S")
+                h_bank(0, 2 * i - 1, "S")
+        load_x(2)
+        load_x(3)
+        nc.sync.dma_start(out=bias_bc[:], in_=bias.partition_broadcast(P))
+        load_x(4)
+        load_x(5)
+        x_bank(1, 0, "S")
+        quant_w("L", 7)
+        for bk in range(1, 4):
+            x_bank(1, bk, "VSV"[bk - 1])
+        h_bank(0, 6, "S")
+        h_bank(0, 7, "S")
+        for i in range(4):
+            for l in (2 * i, 2 * i + 1):
+                w_bank("R", l, 0, "S")
+                w_bank("R", l, 1, "V")
+                quant_w("R", l - 1) if l else quant_x(1)
+            if i == 1:
+                for bk in range(4):
+                    g_bank(0, bk, "SV"[bk % 2])
+            h_bank(1, 2 * i, "S")
+            h_bank(1, 2 * i + 1, "S")
+            if i == 2:
+                quant_g(0)
+        for bk in range(4):
+            x_bank(2, bk, "SV"[bk % 2])
+        load_x(6)
+        quant_w("R", 7)
+        for bk in range(4):
+            x_bank(3, bk, "SV"[bk % 2])
+        load_x(7)
+        quant_x(2)
+
+        for j in range(TILES):
+            for half in range(2):
+                def xs_part():
+                    if j + 4 < TILES:
+                        for bk in (2 * half, 2 * half + 1):
+                            x_bank(j + 4, bk, "S")
+
+                def gs_part():
+                    if j + 1 < TILES:
+                        for bk in (2 * half, 2 * half + 1):
+                            g_bank(j + 1, bk, "SV"[bk % 2])
+
+                for part in ((xs_part, gs_part), (gs_part, xs_part))[half]:
+                    part()
+                if half == 0:
+                    if j + 3 < TILES:
+                        quant_x(j + 3)
+                elif j + 1 < TILES:
+                    quant_g(j + 1)
+                if j + 2 < TILES:
+                    for k in range(4 * half, 4 * half + 4):
+                        h_bank(j + 2, k, "S")
+                for n in range(4 * half, 4 * half + 4):
+                    y_mm(j, n)
+                    y_out(j, n)

@@ -12,6 +12,7 @@ ADD = mybir.AluOpType.add
 
 P = 128
 TILES = 8
+ON_SCALAR = {}
 FLOPS = 2 * 2 * 1024 * 8 * 512 * 512
 
 
@@ -26,7 +27,7 @@ def tile_butterflyblocksparselinear_kernel(tc, x, factorL, factorR, bias, out):
         wpool = ctx.enter_context(tc.tile_pool(name="wpool", bufs=8))
         gpool = ctx.enter_context(tc.tile_pool(name="gpool", bufs=2))
         cpool = ctx.enter_context(tc.tile_pool(name="cpool", bufs=2))
-        opool = ctx.enter_context(tc.tile_pool(name="opool", bufs=6))
+        opool = ctx.enter_context(tc.tile_pool(name="opool", bufs=8))
         psum = ctx.enter_context(tc.psum_pool(name="psum", bufs=8))
 
         ident = const.tile([P, P], F32, name="ident")
@@ -37,6 +38,7 @@ def tile_butterflyblocksparselinear_kernel(tc, x, factorL, factorR, bias, out):
         r_codes = const.tile([P, 8, 512], U32, name="r_codes", align_bytes=64)
         r_scales = const.tile([P, 8, 512], U8, name="r_scales", align_bytes=64)
 
+        deferred, done = [], []
         xraw, xg, xc, xs, hx, hg, gc, gs, ob, wraw, wg, yb = {}, {}, {}, {}, {}, {}, {}, {}, {}, {}, {}, {}
         copy = {"S": nc.scalar.copy, "V": nc.vector.tensor_copy}
 
@@ -164,19 +166,29 @@ def tile_butterflyblocksparselinear_kernel(tc, x, factorL, factorR, bias, out):
             if lh == 0:
                 ob[t, sg] = opool.tile([P, 1024], F32, name="ob")
             cols = slice(4 * lh, 4 * lh + 4)
-            nc.vector.tensor_tensor(
-                out=ob[t, sg][:].rearrange("p (s l) -> p s l", l=8)[:, :, cols],
-                in0=yb[t, n][:].rearrange("p (l s) -> p s l", l=4),
-                in1=bias_bc[:, 1024 * sg : 1024 * sg + 1024].rearrange("p (s l) -> p s l", l=8)[:, :, cols],
-                op=ADD,
-            )
+            dst = ob[t, sg][:].rearrange("p (s l) -> p s l", l=8)[:, :, cols]
+            src = yb[t, n][:].rearrange("p (l s) -> p s l", l=4)
+            row = bias_bc[:, 1024 * sg : 1024 * sg + 1024]
+            if sg in ON_SCALAR.get(t, ()):
+                nc.scalar.copy(out=dst, in_=src)
+                if lh == 1:
+                    nc.gpsimd.tensor_tensor(out=ob[t, sg][:], in0=ob[t, sg][:], in1=row, op=ADD)
+            else:
+                nc.vector.tensor_tensor(
+                    out=dst, in0=src, in1=row.rearrange("p (s l) -> p s l", l=8)[:, :, cols], op=ADD
+                )
             if lh == 1:
-                store(t, sg)
+                if sg in ON_SCALAR.get(t, ()):
+                    deferred.append((t, sg, len(done) + 2))
+                else:
+                    store(t, sg)
+                done.append((t, sg))
+                while deferred and len(done) > deferred[0][2]:
+                    store(*deferred.pop(0)[:2])
 
         load_x(0, 4)
         for k in range(8):
             load_l(k)
-        load_x(1)
         make_identity(nc, ident[:])
         for lh in range(2):
             nc.vector.tensor_copy(
@@ -187,70 +199,74 @@ def tile_butterflyblocksparselinear_kernel(tc, x, factorL, factorR, bias, out):
             x_bank(0, bk, "SV"[bk % 2])
             if bk % 2:
                 quant_x(0, bk // 2)
-        for i in range(4):
-            for k in (2 * i, 2 * i + 1):
-                w_bank("L", k, 0, "S")
-                w_bank("L", k, 1, "V")
-                if k:
-                    quant_w("L", k - 1)
-                load_r(k)
-            if i:
-                h_bank(0, 2 * i - 2, "S")
-                h_bank(0, 2 * i - 1, "S")
+        for k in range(8):
+            w_bank("L", k, 0, "S")
+            w_bank("L", k, 1, "V")
+            if k:
+                quant_w("L", k - 1)
+            load_r(k)
+            if k == 3:
+                load_x(1)
+            if k == 5:
+                for n in range(4):
+                    h_bank(0, n, "S")
         load_x(2)
-        load_x(3)
         nc.sync.dma_start(out=bias_bc[:], in_=bias.partition_broadcast(P))
-        load_x(4)
-        load_x(5)
-        x_bank(1, 0, "S")
-        quant_w("L", 7)
-        for bk in range(1, 4):
-            x_bank(1, bk, "VSV"[bk - 1])
-        h_bank(0, 6, "S")
-        h_bank(0, 7, "S")
-        for i in range(4):
-            for l in (2 * i, 2 * i + 1):
-                w_bank("R", l, 0, "S")
-                w_bank("R", l, 1, "V")
-                quant_w("R", l - 1) if l else quant_x(1)
-            if i == 1:
+        for t in range(3, 6):
+            load_x(t)
+        for l in range(8):
+            w_bank("R", l, 0, "S")
+            w_bank("R", l, 1, "V")
+            quant_w("R", l - 1) if l else quant_w("L", 7)
+            if l == 1:
+                for n in range(4, 8):
+                    h_bank(0, n, "S")
+            if l == 5:
+                for bk in range(4):
+                    x_bank(1, bk, "SV"[bk % 2])
+            if l == 3:
                 for bk in range(4):
                     g_bank(0, bk, "SV"[bk % 2])
-            h_bank(1, 2 * i, "S")
-            h_bank(1, 2 * i + 1, "S")
-            if i == 2:
+            if l == 4:
                 quant_g(0)
+            if l == 6:
+                quant_x(1)
+        quant_w("R", 7)
         for bk in range(4):
             x_bank(2, bk, "SV"[bk % 2])
         load_x(6)
-        quant_w("R", 7)
+        for n in range(4):
+            h_bank(1, n, "S")
+        quant_x(2)
         for bk in range(4):
             x_bank(3, bk, "SV"[bk % 2])
         load_x(7)
-        quant_x(2)
 
         for j in range(TILES):
-            for half in range(2):
-                def xs_part():
-                    if j + 4 < TILES:
-                        for bk in (2 * half, 2 * half + 1):
-                            x_bank(j + 4, bk, "S")
-
-                def gs_part():
-                    if j + 1 < TILES:
-                        for bk in (2 * half, 2 * half + 1):
-                            g_bank(j + 1, bk, "SV"[bk % 2])
-
-                for part in ((xs_part, gs_part), (gs_part, xs_part))[half]:
-                    part()
-                if half == 0:
-                    if j + 3 < TILES:
-                        quant_x(j + 3)
-                elif j + 1 < TILES:
-                    quant_g(j + 1)
+            if j + 1 < TILES:
+                for k in range(4, 8):
+                    h_bank(j + 1, k, "SVSS"[k - 4])
+            for n in range(4):
+                y_mm(j, n)
+                y_out(j, n)
+            if j + 1 < TILES:
+                for bk in range(4):
+                    g_bank(j + 1, bk, "SSSS"[bk] if j + 2 < TILES else "SSSS"[bk])
+            if j + 3 < TILES and 2 == 2:
+                quant_x(j + 3)
+            for n in range(4):
                 if j + 2 < TILES:
-                    for k in range(4 * half, 4 * half + 4):
-                        h_bank(j + 2, k, "S")
-                for n in range(4 * half, 4 * half + 4):
-                    y_mm(j, n)
-                    y_out(j, n)
+                    h_bank(j + 2, n, "SSSS"[n])
+                y_mm(j, n + 4)
+                if n == (4 if j + 4 < TILES else 2) and j + 1 < TILES:
+                    quant_g(j + 1)
+                y_out(j, n + 4)
+            if j + 1 < TILES and (j + 4 < TILES or 2 == 4):
+                quant_g(j + 1)
+            if j + 3 < TILES and 2 == 1:
+                quant_x(j + 3)
+            if j + 3 < TILES and 2 == 0:
+                quant_x(j + 3)
+            if j + 4 < TILES:
+                for bk in range(4):
+                    x_bank(j + 4, bk, "SSSV"[bk])

@@ -201,7 +201,7 @@ def tile_butterflyblocksparselinear_kernel(tc, x, factorL, factorR, bias, out):
                 quant_x(0, bk // 2)
         for k in range(8):
             w_bank("L", k, 0, "S")
-            w_bank("L", k, 1, "V")
+            w_bank("L", k, 1, "SV"[k % 2])
             if k:
                 quant_w("L", k - 1)
             load_r(k)
@@ -216,7 +216,7 @@ def tile_butterflyblocksparselinear_kernel(tc, x, factorL, factorR, bias, out):
             load_x(t)
         for l in range(8):
             w_bank("R", l, 0, "S")
-            w_bank("R", l, 1, "V")
+            w_bank("R", l, 1, "SV"[l % 2])
             quant_w("R", l - 1) if l else quant_w("L", 7)
             if l == 1:
                 for n in range(4, 8):

@@ -235,7 +235,7 @@ def tile_butterflyblocksparselinear_kernel(tc, x, factorL, factorR, bias, out):
         for bk in range(4):
             x_bank(2, bk, "SV"[bk % 2])
         load_x(6)
-        for n in range(4):
+        for n in range(8):
             h_bank(1, n, "S")
         quant_x(2)
         for bk in range(4):
@@ -243,30 +243,25 @@ def tile_butterflyblocksparselinear_kernel(tc, x, factorL, factorR, bias, out):
         load_x(7)
 
         for j in range(TILES):
-            if j + 1 < TILES:
-                for k in range(4, 8):
-                    h_bank(j + 1, k, "SVSS"[k - 4])
             for n in range(4):
+                if j + 2 < TILES:
+                    h_bank(j + 2, n, "S")
                 y_mm(j, n)
                 y_out(j, n)
             if j + 1 < TILES:
                 for bk in range(4):
-                    g_bank(j + 1, bk, "SSSS"[bk] if j + 2 < TILES else "SSSS"[bk])
-            if j + 3 < TILES and 2 == 2:
+                    g_bank(j + 1, bk, "S")
+            if j + 3 < TILES:
                 quant_x(j + 3)
             for n in range(4):
                 if j + 2 < TILES:
-                    h_bank(j + 2, n, "SSSS"[n])
+                    h_bank(j + 2, n + 4, "S")
                 y_mm(j, n + 4)
                 if n == (4 if j + 4 < TILES else 2) and j + 1 < TILES:
                     quant_g(j + 1)
                 y_out(j, n + 4)
-            if j + 1 < TILES and (j + 4 < TILES or 2 == 4):
+            if j + 4 < TILES:
                 quant_g(j + 1)
-            if j + 3 < TILES and 2 == 1:
-                quant_x(j + 3)
-            if j + 3 < TILES and 2 == 0:
-                quant_x(j + 3)
             if j + 4 < TILES:
                 for bk in range(4):
-                    x_bank(j + 4, bk, "SSSV"[bk])
+                    x_bank(j + 4, bk, "SSVV"[bk])

@@ -33,10 +33,10 @@ def tile_butterflyblocksparselinear_kernel(tc, x, factorL, factorR, bias, out):
         ident = const.tile([P, P], F32, name="ident")
         perm = const.tile([P, P], F32, name="perm")
         bias_bc = const.tile([P, 4096], BF16, name="bias_bc")
-        l_codes = const.tile([P, 8, 512], U32, name="l_codes", align_bytes=64)
-        l_scales = const.tile([P, 8, 512], U8, name="l_scales", align_bytes=64)
-        r_codes = const.tile([P, 8, 512], U32, name="r_codes", align_bytes=64)
-        r_scales = const.tile([P, 8, 512], U8, name="r_scales", align_bytes=64)
+        l_codes = const.tile([P, 8, 512], U32, name="l_codes", align_bytes=256)
+        l_scales = const.tile([P, 8, 512], U8, name="l_scales", align_bytes=256)
+        r_codes = const.tile([P, 8, 512], U32, name="r_codes", align_bytes=256)
+        r_scales = const.tile([P, 8, 512], U8, name="r_scales", align_bytes=256)
 
         deferred, done = [], []
         xraw, xg, xc, xs, hx, hg, gc, gs, ob, wraw, wg, yb = {}, {}, {}, {}, {}, {}, {}, {}, {}, {}, {}, {}
@@ -114,8 +114,8 @@ def tile_butterflyblocksparselinear_kernel(tc, x, factorL, factorR, bias, out):
 
         def quant_x(t, half=None):
             if half in (None, 0):
-                xc[t] = cpool.tile([P, 1024], U32, name="xc", align_bytes=64)
-                xs[t] = cpool.tile([P, 1024], U8, name="xs", align_bytes=64)
+                xc[t] = cpool.tile([P, 1024], U32, name="xc", align_bytes=256)
+                xs[t] = cpool.tile([P, 1024], U8, name="xs", align_bytes=256)
             a, b = (0, 1024) if half is None else (512 * half, 512 * half + 512)
             nc.vector.quantize_mx(out=xc[t][:, a:b].bitcast(FP8X4), scales=xs[t][:, a:b], in_=xg[t][:, 4 * a : 4 * b])
 
@@ -124,8 +124,8 @@ def tile_butterflyblocksparselinear_kernel(tc, x, factorL, factorR, bias, out):
             nc.vector.quantize_mx(out=codes[:, j, :].bitcast(FP8X4), scales=scales[:, j, :], in_=wg[kind, j][:])
 
         def quant_g(t):
-            gc[t] = cpool.tile([P, 1024], U32, name="gc", align_bytes=64)
-            gs[t] = cpool.tile([P, 1024], U8, name="gs", align_bytes=64)
+            gc[t] = cpool.tile([P, 1024], U32, name="gc", align_bytes=256)
+            gs[t] = cpool.tile([P, 1024], U8, name="gs", align_bytes=256)
             nc.vector.quantize_mx(out=gc[t][:].bitcast(FP8X4), scales=gs[t][:], in_=hg[t][:])
 
         def h_bank(t, k, eng):

@@ -211,8 +211,9 @@ def tile_butterflyblocksparselinear_kernel(tc, x, factorL, factorR, bias, out):
                 for n in range(4):
                     h_bank(0, n, "S")
         load_x(2)
+        load_x(3)
         nc.sync.dma_start(out=bias_bc[:], in_=bias.partition_broadcast(P))
-        for t in range(3, 6):
+        for t in range(4, 6):
             load_x(t)
         for l in range(8):
             w_bank("R", l, 0, "S")
@@ -233,10 +234,10 @@ def tile_butterflyblocksparselinear_kernel(tc, x, factorL, factorR, bias, out):
                 quant_x(1)
         quant_w("R", 7)
         for bk in range(4):
-            x_bank(2, bk, "SV"[bk % 2])
+            x_bank(2, bk, "S")
         load_x(6)
         for n in range(8):
-            h_bank(1, n, "S")
+            h_bank(1, n, "SV"[n % 2])
         quant_x(2)
         for bk in range(4):
             x_bank(3, bk, "SV"[bk % 2])
@@ -257,7 +258,7 @@ def tile_butterflyblocksparselinear_kernel(tc, x, factorL, factorR, bias, out):
                 if j + 2 < TILES:
                     h_bank(j + 2, n + 4, "S")
                 y_mm(j, n + 4)
-                if n == (4 if j + 4 < TILES else 2) and j + 1 < TILES:
+                if n == (4 if j + 4 < TILES else 1 if j == 4 else 2) and j + 1 < TILES:
                     quant_g(j + 1)
                 y_out(j, n + 4)
             if j + 4 < TILES:

@@ -207,8 +207,8 @@ def tile_butterflyblocksparselinear_kernel(tc, x, factorL, factorR, bias, out):
             load_r(k)
             if k == 3:
                 load_x(1)
-            if k == 5:
-                for n in range(4):
+            if k % 2 and k > 1:
+                for n in (k - 3, k - 2):
                     h_bank(0, n, "S")
         load_x(2)
         load_x(3)
@@ -220,7 +220,7 @@ def tile_butterflyblocksparselinear_kernel(tc, x, factorL, factorR, bias, out):
             w_bank("R", l, 1, "SV"[l % 2])
             quant_w("R", l - 1) if l else quant_w("L", 7)
             if l == 1:
-                for n in range(4, 8):
+                for n in (6, 7):
                     h_bank(0, n, "S")
             if l == 5:
                 for bk in range(4):

from contextlib import ExitStack

import concourse.mybir as mybir
from concourse.masks import make_identity

F32 = mybir.dt.float32
BF16 = mybir.dt.bfloat16
U32 = mybir.dt.uint32
U8 = mybir.dt.uint8
FP8X4 = mybir.dt.float8_e4m3fn_x4
ADD = mybir.AluOpType.add

P = 128
TILES = 8
ON_SCALAR = {}
FLOPS = 2 * 2 * 1024 * 8 * 512 * 512


def tile_butterflyblocksparselinear_kernel(tc, x, factorL, factorR, bias, out):
    nc = tc.nc
    xf = x.flatten_outer_dims()
    of = out.flatten_outer_dims()
    with ExitStack() as ctx:
        ctx.enter_context(tc.manual_schedule())
        const = ctx.enter_context(tc.tile_pool(name="const", bufs=1))
        xpool = ctx.enter_context(tc.tile_pool(name="xpool", bufs=4))
        wpool = ctx.enter_context(tc.tile_pool(name="wpool", bufs=8))
        gpool = ctx.enter_context(tc.tile_pool(name="gpool", bufs=2))
        cpool = ctx.enter_context(tc.tile_pool(name="cpool", bufs=2))
        opool = ctx.enter_context(tc.tile_pool(name="opool", bufs=8))
        psum = ctx.enter_context(tc.psum_pool(name="psum", bufs=8))

        ident = const.tile([P, P], F32, name="ident")
        perm = const.tile([P, P], F32, name="perm")
        bias_bc = const.tile([P, 4096], BF16, name="bias_bc")
        l_codes = const.tile([P, 8, 512], U32, name="l_codes", align_bytes=256)
        l_scales = const.tile([P, 8, 512], U8, name="l_scales", align_bytes=256)
        r_codes = const.tile([P, 8, 512], U32, name="r_codes", align_bytes=256)
        r_scales = const.tile([P, 8, 512], U8, name="r_scales", align_bytes=256)

        deferred, done = [], []
        xraw, xg, xc, xs, hx, hg, gc, gs, ob, wraw, wg, yb = {}, {}, {}, {}, {}, {}, {}, {}, {}, {}, {}, {}
        copy = {"S": nc.scalar.copy, "V": nc.vector.tensor_copy}

        def load_x(t, pieces=1):
            xraw[t] = xpool.tile([P, 4096], BF16, name="xraw")
            w = 4096 // pieces
            for c in range(pieces):
                nc.sync.dma_start(out=xraw[t][:, c * w : c * w + w], in_=xf[t * P : (t + 1) * P, c * w : c * w + w])

        def load_l(k):
            wraw["L", k] = wpool.tile([P, 2048], BF16, name="wraw")
            nc.sync.dma_start(out=wraw["L", k][:], in_=factorL[k].rearrange("(m a) p -> m (a p)", a=4))

        def load_r(l):
            wraw["R", l] = wpool.tile([P, 2048], BF16, name="wraw")
            nc.sync.dma_start(
                out=wraw["R", l][:].rearrange("m (h c) -> m h c", h=2),
                in_=factorR[l].rearrange("(h m b) r -> m h (b r)", h=2, b=2),
            )

        def store(t, sg):
            nc.sync.dma_start(out=of[t * P : (t + 1) * P, 1024 * sg : 1024 * sg + 1024], in_=ob[t, sg][:])

        def x_bank(t, bk, eng):
            if bk == 0:
                xg[t] = gpool.tile([P, 4096], BF16, name="xg", align_bytes=64)
            words = xraw[t][:].bitcast(F32)
            tp = psum.tile([P, 512], F32, name="xp", tag="ps")
            for c in range(4):
                k, u = 2 * bk + c // 2, c % 2
                nc.tensor.transpose(tp[:, c * P : (c + 1) * P], words[:, 256 * k + u : 256 * k + 256 : 2], ident[:])
            copy[eng](
                out=xg[t][:].bitcast(F32)[:, 512 * bk : 512 * bk + 512].rearrange("p (k c u) -> p k c u", k=2, u=2),
                in_=tp[:].rearrange("p (k u c) -> p k c u", k=2, u=2),
            )

        def w_bank(kind, j, half, eng):
            if half == 0:
                wg[kind, j] = gpool.tile([P, 2048], BF16, name="wg", bufs=3, align_bytes=64)
            words = wraw[kind, j][:].bitcast(F32)
            tp = psum.tile([P, 512], F32, name="wp", tag="ps")
            for c in range(4):
                a, u = 2 * half + c // 2, c % 2
                nc.tensor.transpose(
                    tp[:, c * P : (c + 1) * P],
                    words[:, 256 * a + u : 256 * a + 256 : 2],
                    perm[:] if kind == "L" else ident[:],
                )
            dst = wg[kind, j][:].bitcast(F32)[:, 512 * half : 512 * half + 512]
            if kind == "L":
                copy[eng](
                    out=dst.rearrange("p (a n u) -> p a n u", a=2, u=2),
                    in_=tp[:].rearrange("p (a u n) -> p a n u", a=2, u=2),
                )
            else:
                copy[eng](
                    out=dst.rearrange("p (m b u) -> p m b u", b=2, u=2),
                    in_=tp[:].rearrange("p (b u m) -> p m b u", b=2, u=2),
                )

        def g_bank(t, bk, eng):
            if bk == 0:
                hg[t] = gpool.tile([P, 4096], BF16, name="hg", align_bytes=64)
            words = hx[t][:].bitcast(F32)
            tp = psum.tile([P, 512], F32, name="gp", tag="ps")
            for c in range(4):
                n = 4 * bk + c
                nc.tensor.transpose(tp[:, c * P : (c + 1) * P], words[:, n * P : (n + 1) * P], ident[:])
            copy[eng](
                out=hg[t][:].bitcast(F32)[:, 512 * bk : 512 * bk + 512].rearrange("p (l c v) -> p l c v", l=2, v=2),
                in_=tp[:].rearrange("p (l v c) -> p l c v", l=2, v=2),
            )

        def quant_x(t, half=None):
            if half in (None, 0):
                xc[t] = cpool.tile([P, 1024], U32, name="xc", align_bytes=256)
                xs[t] = cpool.tile([P, 1024], U8, name="xs", align_bytes=256)
            a, b = (0, 1024) if half is None else (512 * half, 512 * half + 512)
            nc.vector.quantize_mx(out=xc[t][:, a:b].bitcast(FP8X4), scales=xs[t][:, a:b], in_=xg[t][:, 4 * a : 4 * b])

        def quant_w(kind, j):
            codes, scales = (l_codes, l_scales) if kind == "L" else (r_codes, r_scales)
            nc.vector.quantize_mx(out=codes[:, j, :].bitcast(FP8X4), scales=scales[:, j, :], in_=wg[kind, j][:])

        def quant_g(t):
            gc[t] = cpool.tile([P, 1024], U32, name="gc", align_bytes=256)
            gs[t] = cpool.tile([P, 1024], U8, name="gs", align_bytes=256)
            nc.vector.quantize_mx(out=gc[t][:].bitcast(FP8X4), scales=gs[t][:], in_=hg[t][:])

        def h_bank(t, k, eng):
            if k == 0:
                hx[t] = gpool.tile([P, 4096], BF16, name="hx", align_bytes=64)
            hb = psum.tile([P, 512], F32, name="hb", tag="ps")
            nc.tensor.matmul_mx(
                out=hb[:],
                lhsT=xc[t][:, k * P : (k + 1) * P].bitcast(FP8X4),
                lhsT_scale=xs[t][:, k * P : (k + 1) * P],
                rhs=l_codes[:, k, :].bitcast(FP8X4),
                rhs_scale=l_scales[:, k, :],
                start=True,
                stop=True,
            )
            copy[eng](
                out=hx[t][:].rearrange("p (n k i) -> p n k i", k=8, i=32)[:, :, k, :],
                in_=hb[:].rearrange("p (n i) -> p n i", i=32),
            )

        def y_mm(t, n):
            sg, lh = n // 2, n % 2
            yb[t, n] = psum.tile([P, 512], F32, name="yb", tag="ps")
            for a in range(4):
                c = 2 * a + lh
                nc.tensor.matmul_mx(
                    out=yb[t, n][:, a * P : (a + 1) * P],
                    lhsT=gc[t][:, c * P : (c + 1) * P].bitcast(FP8X4),
                    lhsT_scale=gs[t][:, c * P : (c + 1) * P],
                    rhs=r_codes[:, 4 * lh + a, sg * P : (sg + 1) * P].bitcast(FP8X4),
                    rhs_scale=r_scales[:, 4 * lh + a, sg * P : (sg + 1) * P],
                    start=True,
                    stop=True,
                )

        def y_out(t, n):
            sg, lh = n // 2, n % 2
            if lh == 0:
                ob[t, sg] = opool.tile([P, 1024], F32, name="ob")
            cols = slice(4 * lh, 4 * lh + 4)
            dst = ob[t, sg][:].rearrange("p (s l) -> p s l", l=8)[:, :, cols]
            src = yb[t, n][:].rearrange("p (l s) -> p s l", l=4)
            row = bias_bc[:, 1024 * sg : 1024 * sg + 1024]
            if sg in ON_SCALAR.get(t, ()):
                nc.scalar.copy(out=dst, in_=src)
                if lh == 1:
                    nc.gpsimd.tensor_tensor(out=ob[t, sg][:], in0=ob[t, sg][:], in1=row, op=ADD)
            else:
                nc.vector.tensor_tensor(
                    out=dst, in0=src, in1=row.rearrange("p (s l) -> p s l", l=8)[:, :, cols], op=ADD
                )
            if lh == 1:
                if sg in ON_SCALAR.get(t, ()):
                    deferred.append((t, sg, len(done) + 2))
                else:
                    store(t, sg)
                done.append((t, sg))
                while deferred and len(done) > deferred[0][2]:
                    store(*deferred.pop(0)[:2])

        load_x(0, 4)
        for k in range(8):
            load_l(k)
        make_identity(nc, ident[:])
        for lh in range(2):
            nc.vector.tensor_copy(
                out=perm[:, 64 * lh : 64 * lh + 64].rearrange("p (v i e) -> p v i e", v=2, e=2),
                in_=ident[:].rearrange("p (i v e b) -> p b v i e", v=2, e=2, b=2)[:, lh],
            )
        for bk in range(4):
            x_bank(0, bk, "SV"[bk % 2])
            if bk % 2:
                quant_x(0, bk // 2)
        for k in range(8):
            w_bank("L", k, 0, "S")
            w_bank("L", k, 1, "SV"[k % 2])
            if k:
                quant_w("L", k - 1)
            load_r(k)
            if k == 3:
                load_x(1)
            if k % 2 and k > 1:
                for n in (k - 3, k - 2):
                    h_bank(0, n, "S")
        load_x(2)
        load_x(3)
        nc.sync.dma_start(out=bias_bc[:], in_=bias.partition_broadcast(P))
        for t in range(4, 6):
            load_x(t)
        for l in range(8):
            w_bank("R", l, 0, "S")
            w_bank("R", l, 1, "SV"[l % 2])
            quant_w("R", l - 1) if l else quant_w("L", 7)
            if l == 1:
                for n in (6, 7):
                    h_bank(0, n, "S")
            if l == 5:
                for bk in range(4):
                    x_bank(1, bk, "SV"[bk % 2])
            if l == 3:
                for bk in range(4):
                    g_bank(0, bk, "SV"[bk % 2])
            if l == 4:
                quant_g(0)
            if l == 6:
                quant_x(1)
        quant_w("R", 7)
        for bk in range(4):
            x_bank(2, bk, "S")
        load_x(6)
        for n in range(8):
            h_bank(1, n, "SV"[n % 2])
        quant_x(2)
        for bk in range(4):
            x_bank(3, bk, "SV"[bk % 2])
        load_x(7)

        for j in range(TILES):
            for n in range(4):
                if j + 2 < TILES:
                    h_bank(j + 2, n, "S")
                y_mm(j, n)
                y_out(j, n)
            if j + 1 < TILES:
                for bk in range(4):
                    g_bank(j + 1, bk, "S")
            if j + 3 < TILES:
                quant_x(j + 3)
            for n in range(4):
                if j + 2 < TILES:
                    h_bank(j + 2, n + 4, "S")
                y_mm(j, n + 4)
                if n == (4 if j + 4 < TILES else 1 if j == 4 else 2) and j + 1 < TILES:
                    quant_g(j + 1)
                y_out(j, n + 4)
            if j + 4 < TILES:
                quant_g(j + 1)
            if j + 4 < TILES:
                for bk in range(4):
                    x_bank(j + 4, bk, "SSVV"[bk])
